import numpy as np
import ml_dtypes


def mxq(x, axis, fmt="e4m3"):
    dtype, down = {"e4m3": (ml_dtypes.float8_e4m3fn, 7), "e5m2": (ml_dtypes.float8_e5m2, 14)}[fmt]
    v = np.moveaxis(np.asarray(x, np.float32).astype(ml_dtypes.bfloat16).astype(np.float64), axis, -1)
    blocks = v.reshape(v.shape[:-1] + (-1, 32))
    amax = np.abs(blocks).max(-1, keepdims=True)
    byte = np.maximum(np.where(amax > 0, np.frexp(amax)[1] - 1 + 127, 0) - down, 1)
    scale = np.exp2(byte - 127.0)
    codes = (blocks / scale).astype(np.float32).astype(dtype).astype(np.float64)
    return np.moveaxis((codes * scale).reshape(v.shape), -1, axis)


WIDE = False


def mx_kscale(k):
    if not WIDE:
        return np.ones(k)
    levels = np.array([10, -10, 5, -5, 0])
    a = np.random.permutation(np.resize(levels, k // 512 * 4)).reshape(k // 512, 4)
    idx = np.arange(k)
    return np.exp2(a[idx // 512, idx % 128 // 32])


BF16 = ml_dtypes.bfloat16


def bf(x):
    return np.asarray(x, np.float32).astype(BF16)


def f64(x):
    return np.asarray(x).astype(np.float64)


E2M1 = np.array([0.0, 0.5, 1.0, 1.5, 2.0, 3.0, 4.0, 6.0, -0.0, -0.5, -1.0, -1.5, -2.0, -3.0, -4.0, -6.0])


def pack_weight(w, fmt):
    k, n = w.shape
    w = f64(bf(w)).reshape(k // 32, 32, n)
    amax = np.abs(w).max(1)
    if fmt == "e4m3":
        byte = np.frexp(amax)[1] - 1 + 127 - 7
    else:
        mant, ex = np.frexp(amax / 6.0)
        byte = np.where(mant > 0.5, ex, ex - 1) + 127
    byte = np.clip(np.where(amax > 0, byte, 1), 1, 254)
    scaled = (w * np.exp2(127.0 - byte)[:, None, :]).reshape(k, n).astype(np.float32)
    by_word = np.ascontiguousarray(scaled.reshape(k // 512, 128, 4, n).transpose(0, 1, 3, 2))
    if fmt == "e4m3":
        words = by_word.astype(ml_dtypes.float8_e4m3fn).view(np.uint8)
    else:
        c = by_word.astype(ml_dtypes.float4_e2m1fn).view(np.uint8) & 0xF
        words = c[..., 0::2] | (c[..., 1::2] << 4)
    return np.ascontiguousarray(words), np.ascontiguousarray(byte.astype(np.uint8).reshape(k // 512, 16, n))


def unpack_weight(words, scales, fmt):
    g, p, n, _ = words.shape
    if fmt == "e4m3":
        vals = np.ascontiguousarray(words).view(ml_dtypes.float8_e4m3fn).astype(np.float64)
    else:
        nib = np.empty((g, p, n, 4), np.uint8)
        nib[..., 0::2] = words & 0xF
        nib[..., 1::2] = words >> 4
        vals = E2M1[nib]
    vals = vals * np.repeat(np.exp2(scales.astype(np.float64) - 127.0), 8, axis=1)[..., None]
    return vals.transpose(0, 1, 3, 2).reshape(g * 512, n)

def pack4(w):
    words, scales = pack_weight(w, "e2m1")
    return words.reshape(words.shape[0], 128, -1), scales


def unpack4(words, scales):
    return unpack_weight(words.reshape(words.shape[0], 128, -1, 2), scales, "e2m1")


B, NB, NL, NG, NK = 256, 1024, 1536, 500, 3
N2 = 2 * NB


def setup_inputs():
    s = mx_kscale(N2)
    r = s[:NB]
    Volt = bf(np.random.standard_normal((B, N2)) * s)
    y = np.random.standard_normal((NB, N2)) * 4.0 / np.sqrt(N2) / s[None, :] / r[:, None]
    yc = np.random.standard_normal((NB, N2)) * 4.0 / np.sqrt(N2) / s[None, :] / r[:, None]
    PQ_Loads = bf(np.random.standard_normal((B, N2)))
    PQ_Gens = bf(np.random.standard_normal((B, N2)))
    y_words, y_scales = pack4(np.ascontiguousarray(y.T))
    yc_words, yc_scales = pack4(np.ascontiguousarray(yc.T))
    return {'Volt': Volt,
            'Y_top_words': y_words,
            'Y_top_scales': y_scales,
            'Yconj_top_words': yc_words,
            'Yconj_top_scales': yc_scales,
            'PQ_Loads': PQ_Loads,
            'PQ_Gens': PQ_Gens}


def reference(Volt, Y_top_words, Y_top_scales, Yconj_top_words, Yconj_top_scales, PQ_Loads, PQ_Gens):
    V = f64(Volt)
    Vq = mxq(V, 1, 'e4m3')
    YV = Vq @ unpack4(Y_top_words, Y_top_scales)
    YcV = Vq @ unpack4(Yconj_top_words, Yconj_top_scales)
    out = np.sum(V[:, :NB] * YV, axis=1) + np.sum(V[:, :NB] * YcV, axis=1)
    pq = f64(PQ_Loads) - f64(PQ_Gens)
    return out + np.sum(pq[:, :NB], axis=1) + np.sum(pq[:, NB:], axis=1)

@@ -1,0 +1,192 @@
+from contextlib import ExitStack
+
+import concourse.masks as masks
+import concourse.mybir as mybir
+
+BF16 = mybir.dt.bfloat16
+F32 = mybir.dt.float32
+I32 = mybir.dt.int32
+U8 = mybir.dt.uint8
+U32 = mybir.dt.uint32
+FP8X4 = mybir.dt.float8_e4m3fn_x4
+FP4X4 = mybir.dt.float4_e2m1fn_x4
+ALU = mybir.AluOpType
+COPY = mybir.ActivationFunctionType.Copy
+
+P = 128
+PACK = 4
+K_PASS = P * PACK
+B = 256
+K = 2048
+N = 1024
+N_PASS = 512
+SAMPLE_TILES = B // P
+K_GROUPS = K // K_PASS
+COLUMN_HALVES = N // N_PASS
+WEIGHTS = 2
+PAIRS = PACK // 2
+
+PQ_VECTOR_COLS = 1024
+PQ_SCALAR_COLS = K - PQ_VECTOR_COLS
+
+PART_COLS = 8
+VECTOR_PARTS = 0
+SCALAR_PARTS = PART_COLS
+
+FLOPS = 2 * B * K * N * WEIGHTS
+
+
+def tile_kktloss_pc_kernel(
+    tc, volt, y_words, y_scales, yc_words, yc_scales, pq_loads, pq_gens, out
+):
+    nc = tc.nc
+    with ExitStack() as ctx:
+        keep = ctx.enter_context(tc.tile_pool(name="keep", bufs=1))
+        psum_flip = ctx.enter_context(tc.psum_pool(name="psum_flip", bufs=K_GROUPS))
+        psum_acc = ctx.enter_context(tc.psum_pool(name="psum_acc", bufs=1))
+        ctx.enter_context(tc.manual_schedule())
+
+        volt_sb = keep.tile([P, SAMPLE_TILES, K], BF16)
+        loads_sb = keep.tile([P, SAMPLE_TILES, K], BF16)
+        gens_sb = keep.tile([P, SAMPLE_TILES, K], BF16)
+        w_words = keep.tile([P, WEIGHTS, K_GROUPS, 2 * N], U8, align_bytes=64)
+        w_planes = keep.tile([P, WEIGHTS, K_GROUPS, N], U8, align_bytes=64)
+        volt_t = keep.tile([P, K_GROUPS, B * PACK], BF16, align_bytes=64)
+        v_words = keep.tile([P, K_GROUPS, B], U32, align_bytes=64)
+        v_planes = keep.tile([P, K_GROUPS, B], U8, align_bytes=64)
+        identity = keep.tile([P, P], F32)
+        parts = keep.tile([P, SAMPLE_TILES, 2 * PART_COLS], F32)
+        totals = keep.tile([P, P], F32)
+        total_rows = keep.tile([P, P], F32)
+        products = keep.tile([P, SAMPLE_TILES, COLUMN_HALVES, N_PASS], F32)
+        differences = keep.tile([P, SAMPLE_TILES, PQ_VECTOR_COLS], F32)
+        copies = keep.tile([P, SAMPLE_TILES, 2, PQ_SCALAR_COLS], BF16)
+
+        for w in range(WEIGHTS):
+            nc.vector.memset(w_planes[:, w].bitcast(I32), 0)
+        nc.vector.memset(parts[:], 0.0)
+        nc.vector.memset(totals[:], 0.0)
+        masks.make_identity(nc, identity[:])
+
+        volt_rows = volt.rearrange("(i p) k -> p i k", p=P)
+        for g in range(K_GROUPS):
+            k_cols = slice(K_PASS * g, K_PASS * (g + 1))
+            nc.sync.dma_start(out=volt_sb[:, :, k_cols], in_=volt_rows[:, :, k_cols])
+
+        for w, scales in enumerate((y_scales, yc_scales)):
+            scale_rows = scales.bitcast(I32).rearrange("g q n -> q g n")
+            for q in range(8):
+                first = 32 * (q // 4) + q % 4
+                nc.sync.dma_start(
+                    out=w_planes[first:P:64, w].bitcast(I32), in_=scale_rows[q:16:8]
+                )
+
+        for w, words in enumerate((y_words, yc_words)):
+            for g in range(K_GROUPS):
+                nc.sync.dma_start(
+                    out=w_words[:, w, g, :].bitcast(I32), in_=words[g].bitcast(I32)
+                )
+
+        loads_rows = pq_loads.rearrange("(i p) j -> p i j", p=P)
+        gens_rows = pq_gens.rearrange("(i p) j -> p i j", p=P)
+        for i in range(SAMPLE_TILES):
+            nc.sync.dma_start(out=loads_sb[:, i, :], in_=loads_rows[:, i, :])
+            nc.sync.dma_start(out=gens_sb[:, i, :], in_=gens_rows[:, i, :])
+
+        for g in range(K_GROUPS):
+            flipped = psum_flip.tile([P, SAMPLE_TILES, PAIRS, P], F32, tag="flip")
+            for i in range(SAMPLE_TILES):
+                volt_pairs = volt_sb[:, i, :].bitcast(F32)
+                for u in range(PAIRS):
+                    nc.tensor.transpose(
+                        flipped[:, i, u, :],
+                        volt_pairs[:, K_PASS // 2 * g + u : K_PASS // 2 * (g + 1) : PAIRS],
+                        identity[:],
+                    )
+            side_by_side = (
+                volt_t[:, g, :]
+                .bitcast(F32)
+                .rearrange("p (i b u) -> p i b u", i=SAMPLE_TILES, u=PAIRS)
+            )
+            if g % 2 == 0:
+                nc.vector.tensor_copy(
+                    out=side_by_side, in_=flipped[:].rearrange("p i u b -> p i b u")
+                )
+            else:
+                nc.scalar.copy(
+                    out=side_by_side, in_=flipped[:].rearrange("p i u b -> p i b u")
+                )
+            nc.vector.quantize_mx(
+                out=v_words[:, g, :].bitcast(FP8X4),
+                scales=v_planes[:, g, :],
+                in_=volt_t[:, g, :],
+            )
+
+        acc = {}
+        for i in range(SAMPLE_TILES):
+            for h in range(COLUMN_HALVES):
+                acc[(i, h)] = psum_acc.tile([P, N_PASS], F32, name="acc_%d_%d" % (i, h))
+
+        def mx_pass(i, h, w, g):
+            samples = slice(P * i, P * (i + 1))
+            nc.tensor.matmul_mx(
+                out=acc[(i, h)][:],
+                lhsT=v_words[:, g, samples].bitcast(FP8X4),
+                lhsT_scale=v_planes[:, g, samples],
+                rhs=w_words[:, w, g, 2 * N_PASS * h : 2 * N_PASS * (h + 1)].bitcast(FP4X4),
+                rhs_scale=w_planes[:, w, g, N_PASS * h : N_PASS * (h + 1)],
+                start=(w == 0 and g == 0),
+                stop=(w == WEIGHTS - 1 and g == K_GROUPS - 1),
+            )
+
+        for g in range(K_GROUPS):
+            for i in range(SAMPLE_TILES):
+                for h in range(COLUMN_HALVES):
+                    mx_pass(i, h, 0, g)
+
+        for i in range(SAMPLE_TILES):
+            for h in range(COLUMN_HALVES):
+                for g in range(K_GROUPS):
+                    mx_pass(i, h, 1, g)
+                nc.vector.scalar_tensor_tensor(
+                    out=products[:, i, h, :],
+                    in0=acc[(i, h)][:],
+                    scalar=1.0,
+                    in1=volt_sb[:, i, N_PASS * h : N_PASS * (h + 1)],
+                    op0=ALU.mult,
+                    op1=ALU.mult,
+                    accum_out=parts[:, i, VECTOR_PARTS + h : VECTOR_PARTS + h + 1],
+                )
+            nc.vector.scalar_tensor_tensor(
+                out=differences[:, i, :],
+                in0=loads_sb[:, i, 0:PQ_VECTOR_COLS],
+                scalar=1.0,
+                in1=gens_sb[:, i, 0:PQ_VECTOR_COLS],
+                op0=ALU.mult,
+                op1=ALU.subtract,
+                accum_out=parts[:, i, VECTOR_PARTS + 2 : VECTOR_PARTS + 3],
+            )
+            nc.scalar.activation(
+                out=copies[:, i, 0, :],
+                in_=loads_sb[:, i, PQ_VECTOR_COLS:K],
+                func=COPY,
+                scale=1.0,
+                accum_out=parts[:, i, SCALAR_PARTS : SCALAR_PARTS + 1],
+            )
+            nc.scalar.activation(
+                out=copies[:, i, 1, :],
+                in_=gens_sb[:, i, PQ_VECTOR_COLS:K],
+                func=COPY,
+                scale=-1.0,
+                accum_out=parts[:, i, SCALAR_PARTS + 1 : SCALAR_PARTS + 2],
+            )
+
+        nc.vector.tensor_reduce(
+            out=totals[:, 0:SAMPLE_TILES], in_=parts[:], axis=mybir.AxisListType.X, op=ALU.add
+        )
+        totals_flipped = psum_flip.tile([P, P], F32, tag="flip")
+        nc.tensor.transpose(totals_flipped[:], totals[:], identity[:])
+        nc.vector.tensor_copy(out=total_rows[:], in_=totals_flipped[:])
+        nc.sync.dma_start(
+            out=out.rearrange("(i p) -> i p", p=P), in_=total_rows[0:SAMPLE_TILES, :]
+        )

@@ -26,7 +26,7 @@ COLUMN_HALVES = N // N_PASS
 WEIGHTS = 2
 PAIRS = PACK // 2
 
-PQ_VECTOR_COLS = 1024
+PQ_VECTOR_COLS = 768
 PQ_SCALAR_COLS = K - PQ_VECTOR_COLS
 
 PART_COLS = 8
@@ -69,29 +69,38 @@ def tile_kktloss_pc_kernel(
         masks.make_identity(nc, identity[:])
 
         volt_rows = volt.rearrange("(i p) k -> p i k", p=P)
+        loads_rows = pq_loads.rearrange("(i p) j -> p i j", p=P)
+        gens_rows = pq_gens.rearrange("(i p) j -> p i j", p=P)
+        all_words = (y_words, yc_words)
+        all_scales = (y_scales, yc_scales)
+
+        def load_scales(w):
+            scale_rows = all_scales[w].bitcast(I32).rearrange("g q n -> q g n")
+            for r in range(4):
+                nc.sync.dma_start(
+                    out=w_planes[r:P:32, w].bitcast(I32), in_=scale_rows[r:16:4]
+                )
+
+        def load_words(w, g):
+            nc.sync.dma_start(
+                out=w_words[:, w, g, :].bitcast(I32), in_=all_words[w][g].bitcast(I32)
+            )
+
         for g in range(K_GROUPS):
             k_cols = slice(K_PASS * g, K_PASS * (g + 1))
             nc.sync.dma_start(out=volt_sb[:, :, k_cols], in_=volt_rows[:, :, k_cols])
-
-        for w, scales in enumerate((y_scales, yc_scales)):
-            scale_rows = scales.bitcast(I32).rearrange("g q n -> q g n")
-            for q in range(8):
-                first = 32 * (q // 4) + q % 4
-                nc.sync.dma_start(
-                    out=w_planes[first:P:64, w].bitcast(I32), in_=scale_rows[q:16:8]
-                )
-
-        for w, words in enumerate((y_words, yc_words)):
-            for g in range(K_GROUPS):
-                nc.sync.dma_start(
-                    out=w_words[:, w, g, :].bitcast(I32), in_=words[g].bitcast(I32)
-                )
-
-        loads_rows = pq_loads.rearrange("(i p) j -> p i j", p=P)
-        gens_rows = pq_gens.rearrange("(i p) j -> p i j", p=P)
-        for i in range(SAMPLE_TILES):
-            nc.sync.dma_start(out=loads_sb[:, i, :], in_=loads_rows[:, i, :])
-            nc.sync.dma_start(out=gens_sb[:, i, :], in_=gens_rows[:, i, :])
+        load_scales(0)
+        load_words(0, 0)
+        load_words(0, 1)
+        nc.sync.dma_start(out=loads_sb[:, 0, :], in_=loads_rows[:, 0, :])
+        load_words(0, 2)
+        load_words(0, 3)
+        load_scales(1)
+        nc.sync.dma_start(out=gens_sb[:, 0, :], in_=gens_rows[:, 0, :])
+        for g in range(K_GROUPS):
+            load_words(1, g)
+        nc.sync.dma_start(out=loads_sb[:, 1, :], in_=loads_rows[:, 1, :])
+        nc.sync.dma_start(out=gens_sb[:, 1, :], in_=gens_rows[:, 1, :])
 
         for g in range(K_GROUPS):
             flipped = psum_flip.tile([P, SAMPLE_TILES, PAIRS, P], F32, tag="flip")
@@ -139,24 +148,7 @@ def tile_kktloss_pc_kernel(
                 stop=(w == WEIGHTS - 1 and g == K_GROUPS - 1),
             )
 
-        for g in range(K_GROUPS):
-            for i in range(SAMPLE_TILES):
-                for h in range(COLUMN_HALVES):
-                    mx_pass(i, h, 0, g)
-
-        for i in range(SAMPLE_TILES):
-            for h in range(COLUMN_HALVES):
-                for g in range(K_GROUPS):
-                    mx_pass(i, h, 1, g)
-                nc.vector.scalar_tensor_tensor(
-                    out=products[:, i, h, :],
-                    in0=acc[(i, h)][:],
-                    scalar=1.0,
-                    in1=volt_sb[:, i, N_PASS * h : N_PASS * (h + 1)],
-                    op0=ALU.mult,
-                    op1=ALU.mult,
-                    accum_out=parts[:, i, VECTOR_PARTS + h : VECTOR_PARTS + h + 1],
-                )
+        def sum_loads_minus_gens(i):
             nc.vector.scalar_tensor_tensor(
                 out=differences[:, i, :],
                 in0=loads_sb[:, i, 0:PQ_VECTOR_COLS],
@@ -180,6 +172,27 @@ def tile_kktloss_pc_kernel(
                 scale=-1.0,
                 accum_out=parts[:, i, SCALAR_PARTS + 1 : SCALAR_PARTS + 2],
             )
+
+        for g in range(K_GROUPS):
+            for i in range(SAMPLE_TILES):
+                for h in range(COLUMN_HALVES):
+                    mx_pass(i, h, 0, g)
+        sum_loads_minus_gens(0)
+
+        for i in range(SAMPLE_TILES):
+            for h in range(COLUMN_HALVES):
+                for g in range(K_GROUPS):
+                    mx_pass(i, h, 1, g)
+                nc.vector.scalar_tensor_tensor(
+                    out=products[:, i, h, :],
+                    in0=acc[(i, h)][:],
+                    scalar=1.0,
+                    in1=volt_sb[:, i, N_PASS * h : N_PASS * (h + 1)],
+                    op0=ALU.mult,
+                    op1=ALU.mult,
+                    accum_out=parts[:, i, VECTOR_PARTS + h : VECTOR_PARTS + h + 1],
+                )
+        sum_loads_minus_gens(1)
 
         nc.vector.tensor_reduce(
             out=totals[:, 0:SAMPLE_TILES], in_=parts[:], axis=mybir.AxisListType.X, op=ALU.add

@@ -20,6 +20,7 @@ B = 256
 K = 2048
 N = 1024
 N_PASS = 512
+assert N_PASS == K_PASS
 SAMPLE_TILES = B // P
 K_GROUPS = K // K_PASS
 COLUMN_HALVES = N // N_PASS
@@ -46,11 +47,14 @@ def tile_kktloss_pc_kernel(
         psum_acc = ctx.enter_context(tc.psum_pool(name="psum_acc", bufs=1))
         ctx.enter_context(tc.manual_schedule())
 
-        volt_sb = keep.tile([P, SAMPLE_TILES, K], BF16)
+        volt_sb = keep.tile([P, K_GROUPS, SAMPLE_TILES, K_PASS], BF16)
         loads_sb = keep.tile([P, SAMPLE_TILES, K], BF16)
         gens_sb = keep.tile([P, SAMPLE_TILES, K], BF16)
         w_words = keep.tile([P, WEIGHTS, K_GROUPS, 2 * N], U8, align_bytes=64)
-        w_planes = keep.tile([P, WEIGHTS, K_GROUPS, N], U8, align_bytes=64)
+        w_planes = [
+            keep.tile([P, K_GROUPS, N], U8, align_bytes=64, name="w_planes_%d" % w)
+            for w in range(WEIGHTS)
+        ]
         volt_t = keep.tile([P, K_GROUPS, B * PACK], BF16, align_bytes=64)
         v_words = keep.tile([P, K_GROUPS, B], U32, align_bytes=64)
         v_planes = keep.tile([P, K_GROUPS, B], U8, align_bytes=64)
@@ -63,7 +67,7 @@ def tile_kktloss_pc_kernel(
         copies = keep.tile([P, SAMPLE_TILES, 2, PQ_SCALAR_COLS], BF16)
 
         for w in range(WEIGHTS):
-            nc.vector.memset(w_planes[:, w].bitcast(I32), 0)
+            nc.vector.memset(w_planes[w][:].bitcast(I32), 0)
         nc.vector.memset(parts[:], 0.0)
         nc.vector.memset(totals[:], 0.0)
         masks.make_identity(nc, identity[:])
@@ -78,7 +82,7 @@ def tile_kktloss_pc_kernel(
             scale_rows = all_scales[w].bitcast(I32).rearrange("g q n -> q g n")
             for r in range(4):
                 nc.sync.dma_start(
-                    out=w_planes[r:P:32, w].bitcast(I32), in_=scale_rows[r:16:4]
+                    out=w_planes[w][r:P:32].bitcast(I32), in_=scale_rows[r:16:4]
                 )
 
         def load_words(w, g):
@@ -88,7 +92,7 @@ def tile_kktloss_pc_kernel(
 
         for g in range(K_GROUPS):
             k_cols = slice(K_PASS * g, K_PASS * (g + 1))
-            nc.sync.dma_start(out=volt_sb[:, :, k_cols], in_=volt_rows[:, :, k_cols])
+            nc.sync.dma_start(out=volt_sb[:, g], in_=volt_rows[:, :, k_cols])
         load_scales(0)
         load_words(0, 0)
         load_words(0, 1)
@@ -105,12 +109,10 @@ def tile_kktloss_pc_kernel(
         for g in range(K_GROUPS):
             flipped = psum_flip.tile([P, SAMPLE_TILES, PAIRS, P], F32, tag="flip")
             for i in range(SAMPLE_TILES):
-                volt_pairs = volt_sb[:, i, :].bitcast(F32)
+                volt_pairs = volt_sb[:, g, i, :].bitcast(F32)
                 for u in range(PAIRS):
                     nc.tensor.transpose(
-                        flipped[:, i, u, :],
-                        volt_pairs[:, K_PASS // 2 * g + u : K_PASS // 2 * (g + 1) : PAIRS],
-                        identity[:],
+                        flipped[:, i, u, :], volt_pairs[:, u : K_PASS // 2 : PAIRS], identity[:]
                     )
             side_by_side = (
                 volt_t[:, g, :]
@@ -143,7 +145,7 @@ def tile_kktloss_pc_kernel(
                 lhsT=v_words[:, g, samples].bitcast(FP8X4),
                 lhsT_scale=v_planes[:, g, samples],
                 rhs=w_words[:, w, g, 2 * N_PASS * h : 2 * N_PASS * (h + 1)].bitcast(FP4X4),
-                rhs_scale=w_planes[:, w, g, N_PASS * h : N_PASS * (h + 1)],
+                rhs_scale=w_planes[w][:, g, N_PASS * h : N_PASS * (h + 1)],
                 start=(w == 0 and g == 0),
                 stop=(w == WEIGHTS - 1 and g == K_GROUPS - 1),
             )
@@ -187,7 +189,7 @@ def tile_kktloss_pc_kernel(
                     out=products[:, i, h, :],
                     in0=acc[(i, h)][:],
                     scalar=1.0,
-                    in1=volt_sb[:, i, N_PASS * h : N_PASS * (h + 1)],
+                    in1=volt_sb[:, h, i, :],
                     op0=ALU.mult,
                     op1=ALU.mult,
                     accum_out=parts[:, i, VECTOR_PARTS + h : VECTOR_PARTS + h + 1],

@@ -30,6 +30,8 @@ PAIRS = PACK // 2
 PQ_VECTOR_COLS = 768
 PQ_SCALAR_COLS = K - PQ_VECTOR_COLS
 
+BANKWISE_LOADS = 2
+
 PART_COLS = 8
 VECTOR_PARTS = 0
 SCALAR_PARTS = PART_COLS
@@ -175,16 +177,18 @@ def tile_kktloss_pc_kernel(
                 accum_out=parts[:, i, SCALAR_PARTS + 1 : SCALAR_PARTS + 2],
             )
 
-        for g in range(K_GROUPS):
+        landed = [(w, g) for w in range(WEIGHTS) for g in range(K_GROUPS)]
+
+        for w, g in landed[:-BANKWISE_LOADS]:
             for i in range(SAMPLE_TILES):
                 for h in range(COLUMN_HALVES):
-                    mx_pass(i, h, 0, g)
+                    mx_pass(i, h, w, g)
         sum_loads_minus_gens(0)
 
         for i in range(SAMPLE_TILES):
             for h in range(COLUMN_HALVES):
-                for g in range(K_GROUPS):
-                    mx_pass(i, h, 1, g)
+                for w, g in landed[-BANKWISE_LOADS:]:
+                    mx_pass(i, h, w, g)
                 nc.vector.scalar_tensor_tensor(
                     out=products[:, i, h, :],
                     in0=acc[(i, h)][:],

@@ -27,10 +27,9 @@ COLUMN_HALVES = N // N_PASS
 WEIGHTS = 2
 PAIRS = PACK // 2
 
-PQ_VECTOR_COLS = 768
-PQ_SCALAR_COLS = K - PQ_VECTOR_COLS
+PQ_VECTOR_COLS = (768, 512)
 
-BANKWISE_LOADS = 2
+BANKWISE_LOADS = 3
 
 PART_COLS = 8
 VECTOR_PARTS = 0
@@ -65,8 +64,8 @@ def tile_kktloss_pc_kernel(
         totals = keep.tile([P, P], F32)
         total_rows = keep.tile([P, P], F32)
         products = keep.tile([P, SAMPLE_TILES, COLUMN_HALVES, N_PASS], F32)
-        differences = keep.tile([P, SAMPLE_TILES, PQ_VECTOR_COLS], F32)
-        copies = keep.tile([P, SAMPLE_TILES, 2, PQ_SCALAR_COLS], BF16)
+        differences = keep.tile([P, SAMPLE_TILES, K], F32)
+        copies = keep.tile([P, SAMPLE_TILES, 2, K], BF16)
 
         for w in range(WEIGHTS):
             nc.vector.memset(w_planes[w][:].bitcast(I32), 0)
@@ -153,25 +152,26 @@ def tile_kktloss_pc_kernel(
             )
 
         def sum_loads_minus_gens(i):
+            cv = PQ_VECTOR_COLS[i]
             nc.vector.scalar_tensor_tensor(
-                out=differences[:, i, :],
-                in0=loads_sb[:, i, 0:PQ_VECTOR_COLS],
+                out=differences[:, i, 0:cv],
+                in0=loads_sb[:, i, 0:cv],
                 scalar=1.0,
-                in1=gens_sb[:, i, 0:PQ_VECTOR_COLS],
+                in1=gens_sb[:, i, 0:cv],
                 op0=ALU.mult,
                 op1=ALU.subtract,
                 accum_out=parts[:, i, VECTOR_PARTS + 2 : VECTOR_PARTS + 3],
             )
             nc.scalar.activation(
-                out=copies[:, i, 0, :],
-                in_=loads_sb[:, i, PQ_VECTOR_COLS:K],
+                out=copies[:, i, 0, cv:K],
+                in_=loads_sb[:, i, cv:K],
                 func=COPY,
                 scale=1.0,
                 accum_out=parts[:, i, SCALAR_PARTS : SCALAR_PARTS + 1],
             )
             nc.scalar.activation(
-                out=copies[:, i, 1, :],
-                in_=gens_sb[:, i, PQ_VECTOR_COLS:K],
+                out=copies[:, i, 1, cv:K],
+                in_=gens_sb[:, i, cv:K],
                 func=COPY,
                 scale=-1.0,
                 accum_out=parts[:, i, SCALAR_PARTS + 1 : SCALAR_PARTS + 2],
@@ -186,6 +186,8 @@ def tile_kktloss_pc_kernel(
         sum_loads_minus_gens(0)
 
         for i in range(SAMPLE_TILES):
+            if i == 1:
+                sum_loads_minus_gens(1)
             for h in range(COLUMN_HALVES):
                 for w, g in landed[-BANKWISE_LOADS:]:
                     mx_pass(i, h, w, g)
@@ -198,7 +200,6 @@ def tile_kktloss_pc_kernel(
                     op1=ALU.mult,
                     accum_out=parts[:, i, VECTOR_PARTS + h : VECTOR_PARTS + h + 1],
                 )
-        sum_loads_minus_gens(1)
 
         nc.vector.tensor_reduce(
             out=totals[:, 0:SAMPLE_TILES], in_=parts[:], axis=mybir.AxisListType.X, op=ALU.add

@@ -48,7 +48,8 @@ def tile_kktloss_pc_kernel(
         psum_acc = ctx.enter_context(tc.psum_pool(name="psum_acc", bufs=1))
         ctx.enter_context(tc.manual_schedule())
 
-        volt_sb = keep.tile([P, K_GROUPS, SAMPLE_TILES, K_PASS], BF16)
+        volt_sb = keep.tile([P, 2, SAMPLE_TILES, K_PASS], BF16)
+        volt_hi = keep.tile([P, SAMPLE_TILES, 2 * K_PASS], BF16)
         loads_sb = keep.tile([P, SAMPLE_TILES, K], BF16)
         gens_sb = keep.tile([P, SAMPLE_TILES, K], BF16)
         w_words = keep.tile([P, WEIGHTS, K_GROUPS, 2 * N], U8, align_bytes=64)
@@ -88,29 +89,32 @@ def tile_kktloss_pc_kernel(
 
         def load_words(w, g):
             nc.sync.dma_start(
-                out=w_words[:, w, g, :].bitcast(I32), in_=all_words[w][g].bitcast(I32)
+                out=w_words[:, w, g : g + 2, :].bitcast(I32),
+                in_=all_words[w].bitcast(I32)[g : g + 2].rearrange("g p n -> p g n"),
             )
 
-        for g in range(K_GROUPS):
+        for g in range(2):
             k_cols = slice(K_PASS * g, K_PASS * (g + 1))
             nc.sync.dma_start(out=volt_sb[:, g], in_=volt_rows[:, :, k_cols])
+        nc.sync.dma_start(out=volt_hi[:], in_=volt_rows[:, :, 2 * K_PASS : K])
         load_scales(0)
         load_words(0, 0)
-        load_words(0, 1)
-        nc.sync.dma_start(out=loads_sb[:, 0, :], in_=loads_rows[:, 0, :])
         load_words(0, 2)
-        load_words(0, 3)
+        nc.sync.dma_start(out=loads_sb[:, 0, :], in_=loads_rows[:, 0, :])
         load_scales(1)
+        load_words(1, 0)
         nc.sync.dma_start(out=gens_sb[:, 0, :], in_=gens_rows[:, 0, :])
-        for g in range(K_GROUPS):
-            load_words(1, g)
+        load_words(1, 2)
         nc.sync.dma_start(out=loads_sb[:, 1, :], in_=loads_rows[:, 1, :])
         nc.sync.dma_start(out=gens_sb[:, 1, :], in_=gens_rows[:, 1, :])
 
         for g in range(K_GROUPS):
             flipped = psum_flip.tile([P, SAMPLE_TILES, PAIRS, P], F32, tag="flip")
             for i in range(SAMPLE_TILES):
-                volt_pairs = volt_sb[:, g, i, :].bitcast(F32)
+                if g < 2:
+                    volt_pairs = volt_sb[:, g, i, :].bitcast(F32)
+                else:
+                    volt_pairs = volt_hi[:, i, K_PASS * (g - 2) : K_PASS * (g - 1)].bitcast(F32)
                 for u in range(PAIRS):
                     nc.tensor.transpose(
                         flipped[:, i, u, :], volt_pairs[:, u : K_PASS // 2 : PAIRS], identity[:]

@@ -27,13 +27,17 @@ COLUMN_HALVES = N // N_PASS
 WEIGHTS = 2
 PAIRS = PACK // 2
 
-PQ_VECTOR_COLS = (768, 512)
+PQ_VECTOR_COLS = (1280, 576)
+PQ_CUT = 1024
 
 BANKWISE_LOADS = 3
 
 PART_COLS = 8
 VECTOR_PARTS = 0
 SCALAR_PARTS = PART_COLS
+
+WARM_UP_FIRST = 4
+WARM_UP_MID = 2
 
 FLOPS = 2 * B * K * N * WEIGHTS
 
@@ -68,11 +72,19 @@ def tile_kktloss_pc_kernel(
         differences = keep.tile([P, SAMPLE_TILES, K], F32)
         copies = keep.tile([P, SAMPLE_TILES, 2, K], BF16)
 
+        nc.vector.memset(totals[:], 0.0)
         for w in range(WEIGHTS):
             nc.vector.memset(w_planes[w][:].bitcast(I32), 0)
         nc.vector.memset(parts[:], 0.0)
-        nc.vector.memset(totals[:], 0.0)
         masks.make_identity(nc, identity[:])
+
+        warm_up = psum_flip.tile([P, P], F32, tag="flip")
+
+        def keep_warm(count):
+            for n_warm in range(count):
+                nc.tensor.matmul(warm_up[:], lhsT=totals[:], rhs=totals[:], start=True, stop=True)
+
+        keep_warm(WARM_UP_FIRST)
 
         volt_rows = volt.rearrange("(i p) k -> p i k", p=P)
         loads_rows = pq_loads.rearrange("(i p) j -> p i j", p=P)
@@ -105,10 +117,13 @@ def tile_kktloss_pc_kernel(
         load_words(1, 0)
         nc.sync.dma_start(out=gens_sb[:, 0, :], in_=gens_rows[:, 0, :])
         load_words(1, 2)
-        nc.sync.dma_start(out=loads_sb[:, 1, :], in_=loads_rows[:, 1, :])
-        nc.sync.dma_start(out=gens_sb[:, 1, :], in_=gens_rows[:, 1, :])
+        for cols in (slice(0, PQ_CUT), slice(PQ_CUT, K)):
+            nc.sync.dma_start(out=loads_sb[:, 1, cols], in_=loads_rows[:, 1, cols])
+            nc.sync.dma_start(out=gens_sb[:, 1, cols], in_=gens_rows[:, 1, cols])
 
         for g in range(K_GROUPS):
+            if g == 2:
+                keep_warm(WARM_UP_MID)
             flipped = psum_flip.tile([P, SAMPLE_TILES, PAIRS, P], F32, tag="flip")
             for i in range(SAMPLE_TILES):
                 if g < 2:
@@ -155,30 +170,24 @@ def tile_kktloss_pc_kernel(
                 stop=(w == WEIGHTS - 1 and g == K_GROUPS - 1),
             )
 
-        def sum_loads_minus_gens(i):
-            cv = PQ_VECTOR_COLS[i]
+        def pq_vector(i, c0, c1, slot):
             nc.vector.scalar_tensor_tensor(
-                out=differences[:, i, 0:cv],
-                in0=loads_sb[:, i, 0:cv],
+                out=differences[:, i, c0:c1],
+                in0=loads_sb[:, i, c0:c1],
                 scalar=1.0,
-                in1=gens_sb[:, i, 0:cv],
+                in1=gens_sb[:, i, c0:c1],
                 op0=ALU.mult,
                 op1=ALU.subtract,
-                accum_out=parts[:, i, VECTOR_PARTS + 2 : VECTOR_PARTS + 3],
+                accum_out=parts[:, i, VECTOR_PARTS + slot : VECTOR_PARTS + slot + 1],
             )
+
+        def pq_scalar(which, i, c0, c1, slot):
             nc.scalar.activation(
-                out=copies[:, i, 0, cv:K],
-                in_=loads_sb[:, i, cv:K],
+                out=copies[:, i, which, c0:c1],
+                in_=(loads_sb, gens_sb)[which][:, i, c0:c1],
                 func=COPY,
-                scale=1.0,
-                accum_out=parts[:, i, SCALAR_PARTS : SCALAR_PARTS + 1],
-            )
-            nc.scalar.activation(
-                out=copies[:, i, 1, cv:K],
-                in_=gens_sb[:, i, cv:K],
-                func=COPY,
-                scale=-1.0,
-                accum_out=parts[:, i, SCALAR_PARTS + 1 : SCALAR_PARTS + 2],
+                scale=(1.0, -1.0)[which],
+                accum_out=parts[:, i, SCALAR_PARTS + slot : SCALAR_PARTS + slot + 1],
             )
 
         landed = [(w, g) for w in range(WEIGHTS) for g in range(K_GROUPS)]
@@ -187,11 +196,16 @@ def tile_kktloss_pc_kernel(
             for i in range(SAMPLE_TILES):
                 for h in range(COLUMN_HALVES):
                     mx_pass(i, h, w, g)
-        sum_loads_minus_gens(0)
+        cv0, cv1 = PQ_VECTOR_COLS
+        pq_vector(0, 0, cv0, 2)
+        pq_scalar(0, 0, cv0, K, 0)
+        pq_scalar(1, 0, cv0, K, 1)
+        pq_scalar(0, 1, cv1, PQ_CUT, 2)
+        pq_scalar(1, 1, cv1, PQ_CUT, 3)
+        pq_scalar(0, 1, PQ_CUT, K, 4)
+        pq_scalar(1, 1, PQ_CUT, K, 5)
 
         for i in range(SAMPLE_TILES):
-            if i == 1:
-                sum_loads_minus_gens(1)
             for h in range(COLUMN_HALVES):
                 for w, g in landed[-BANKWISE_LOADS:]:
                     mx_pass(i, h, w, g)
@@ -204,6 +218,8 @@ def tile_kktloss_pc_kernel(
                     op1=ALU.mult,
                     accum_out=parts[:, i, VECTOR_PARTS + h : VECTOR_PARTS + h + 1],
                 )
+                if (i, h) == (0, 0):
+                    pq_vector(1, 0, cv1, 2)
 
         nc.vector.tensor_reduce(
             out=totals[:, 0:SAMPLE_TILES], in_=parts[:], axis=mybir.AxisListType.X, op=ALU.add

@@ -37,7 +37,6 @@ VECTOR_PARTS = 0
 SCALAR_PARTS = PART_COLS
 
 WARM_UP_FIRST = 4
-WARM_UP_MID = 2
 
 FLOPS = 2 * B * K * N * WEIGHTS
 
@@ -52,8 +51,7 @@ def tile_kktloss_pc_kernel(
         psum_acc = ctx.enter_context(tc.psum_pool(name="psum_acc", bufs=1))
         ctx.enter_context(tc.manual_schedule())
 
-        volt_sb = keep.tile([P, 2, SAMPLE_TILES, K_PASS], BF16)
-        volt_hi = keep.tile([P, SAMPLE_TILES, 2 * K_PASS], BF16)
+        volt_sb = keep.tile([P, SAMPLE_TILES, K], BF16)
         loads_sb = keep.tile([P, SAMPLE_TILES, K], BF16)
         gens_sb = keep.tile([P, SAMPLE_TILES, K], BF16)
         w_words = keep.tile([P, WEIGHTS, K_GROUPS, 2 * N], U8, align_bytes=64)
@@ -61,9 +59,9 @@ def tile_kktloss_pc_kernel(
             keep.tile([P, K_GROUPS, N], U8, align_bytes=64, name="w_planes_%d" % w)
             for w in range(WEIGHTS)
         ]
-        volt_t = keep.tile([P, K_GROUPS, B * PACK], BF16, align_bytes=64)
-        v_words = keep.tile([P, K_GROUPS, B], U32, align_bytes=64)
-        v_planes = keep.tile([P, K_GROUPS, B], U8, align_bytes=64)
+        volt_t = keep.tile([P, SAMPLE_TILES, K_GROUPS, P * PACK], BF16, align_bytes=64)
+        v_words = keep.tile([P, SAMPLE_TILES, K_GROUPS, P], U32, align_bytes=64)
+        v_planes = keep.tile([P, SAMPLE_TILES, K_GROUPS, P], U8, align_bytes=64)
         identity = keep.tile([P, P], F32)
         parts = keep.tile([P, SAMPLE_TILES, 2 * PART_COLS], F32)
         totals = keep.tile([P, P], F32)
@@ -105,10 +103,9 @@ def tile_kktloss_pc_kernel(
                 in_=all_words[w].bitcast(I32)[g : g + 2].rearrange("g p n -> p g n"),
             )
 
-        for g in range(2):
-            k_cols = slice(K_PASS * g, K_PASS * (g + 1))
-            nc.sync.dma_start(out=volt_sb[:, g], in_=volt_rows[:, :, k_cols])
-        nc.sync.dma_start(out=volt_hi[:], in_=volt_rows[:, :, 2 * K_PASS : K])
+        nc.sync.dma_start(out=volt_sb[:, 0, 0 : K // 2], in_=volt_rows[:, 0, 0 : K // 2])
+        nc.sync.dma_start(out=volt_sb[:, 0, K // 2 : K], in_=volt_rows[:, 0, K // 2 : K])
+        nc.sync.dma_start(out=volt_sb[:, 1, :], in_=volt_rows[:, 1, :])
         load_scales(0)
         load_words(0, 0)
         load_words(0, 2)
@@ -121,36 +118,31 @@ def tile_kktloss_pc_kernel(
             nc.sync.dma_start(out=loads_sb[:, 1, cols], in_=loads_rows[:, 1, cols])
             nc.sync.dma_start(out=gens_sb[:, 1, cols], in_=gens_rows[:, 1, cols])
 
-        for g in range(K_GROUPS):
-            if g == 2:
-                keep_warm(WARM_UP_MID)
-            flipped = psum_flip.tile([P, SAMPLE_TILES, PAIRS, P], F32, tag="flip")
-            for i in range(SAMPLE_TILES):
-                if g < 2:
-                    volt_pairs = volt_sb[:, g, i, :].bitcast(F32)
-                else:
-                    volt_pairs = volt_hi[:, i, K_PASS * (g - 2) : K_PASS * (g - 1)].bitcast(F32)
+        for n in range(SAMPLE_TILES * 2):
+            i, g0 = n // 2, 2 * (n % 2)
+            flipped = psum_flip.tile([P, 2, PAIRS, P], F32, tag="flip")
+            for gg in range(2):
+                g = g0 + gg
+                volt_pairs = volt_sb[:, i, K_PASS * g : K_PASS * (g + 1)].bitcast(F32)
                 for u in range(PAIRS):
                     nc.tensor.transpose(
-                        flipped[:, i, u, :], volt_pairs[:, u : K_PASS // 2 : PAIRS], identity[:]
+                        flipped[:, gg, u, :], volt_pairs[:, u : K_PASS // 2 : PAIRS], identity[:]
                     )
             side_by_side = (
-                volt_t[:, g, :]
-                .bitcast(F32)
-                .rearrange("p (i b u) -> p i b u", i=SAMPLE_TILES, u=PAIRS)
+                volt_t[:, i, g0 : g0 + 2, :].bitcast(F32).rearrange("p g (b u) -> p g b u", u=PAIRS)
             )
-            if g % 2 == 0:
+            if n % 2 == 0:
                 nc.vector.tensor_copy(
-                    out=side_by_side, in_=flipped[:].rearrange("p i u b -> p i b u")
+                    out=side_by_side, in_=flipped[:].rearrange("p g u b -> p g b u")
                 )
             else:
                 nc.scalar.copy(
-                    out=side_by_side, in_=flipped[:].rearrange("p i u b -> p i b u")
+                    out=side_by_side, in_=flipped[:].rearrange("p g u b -> p g b u")
                 )
             nc.vector.quantize_mx(
-                out=v_words[:, g, :].bitcast(FP8X4),
-                scales=v_planes[:, g, :],
-                in_=volt_t[:, g, :],
+                out=v_words[:, i, g0 : g0 + 2, :].rearrange("p g b -> p (g b)").bitcast(FP8X4),
+                scales=v_planes[:, i, g0 : g0 + 2, :].rearrange("p g b -> p (g b)"),
+                in_=volt_t[:, i, g0 : g0 + 2, :].rearrange("p g c -> p (g c)"),
             )
 
         acc = {}
@@ -159,11 +151,10 @@ def tile_kktloss_pc_kernel(
                 acc[(i, h)] = psum_acc.tile([P, N_PASS], F32, name="acc_%d_%d" % (i, h))
 
         def mx_pass(i, h, w, g):
-            samples = slice(P * i, P * (i + 1))
             nc.tensor.matmul_mx(
                 out=acc[(i, h)][:],
-                lhsT=v_words[:, g, samples].bitcast(FP8X4),
-                lhsT_scale=v_planes[:, g, samples],
+                lhsT=v_words[:, i, g, :].bitcast(FP8X4),
+                lhsT_scale=v_planes[:, i, g, :],
                 rhs=w_words[:, w, g, 2 * N_PASS * h : 2 * N_PASS * (h + 1)].bitcast(FP4X4),
                 rhs_scale=w_planes[w][:, g, N_PASS * h : N_PASS * (h + 1)],
                 start=(w == 0 and g == 0),
@@ -213,7 +204,7 @@ def tile_kktloss_pc_kernel(
                     out=products[:, i, h, :],
                     in0=acc[(i, h)][:],
                     scalar=1.0,
-                    in1=volt_sb[:, h, i, :],
+                    in1=volt_sb[:, i, N_PASS * h : N_PASS * (h + 1)],
                     op0=ALU.mult,
                     op1=ALU.mult,
                     accum_out=parts[:, i, VECTOR_PARTS + h : VECTOR_PARTS + h + 1],

@@ -36,8 +36,6 @@ PART_COLS = 8
 VECTOR_PARTS = 0
 SCALAR_PARTS = PART_COLS
 
-WARM_UP_FIRST = 4
-
 FLOPS = 2 * B * K * N * WEIGHTS
 
 
@@ -76,13 +74,6 @@ def tile_kktloss_pc_kernel(
         nc.vector.memset(parts[:], 0.0)
         masks.make_identity(nc, identity[:])
 
-        warm_up = psum_flip.tile([P, P], F32, tag="flip")
-
-        def keep_warm(count):
-            for n_warm in range(count):
-                nc.tensor.matmul(warm_up[:], lhsT=totals[:], rhs=totals[:], start=True, stop=True)
-
-        keep_warm(WARM_UP_FIRST)
 
         volt_rows = volt.rearrange("(i p) k -> p i k", p=P)
         loads_rows = pq_loads.rearrange("(i p) j -> p i j", p=P)

@@ -88,17 +88,18 @@ def tile_kktloss_pc_kernel(
                     out=w_planes[w][r:P:32].bitcast(I32), in_=scale_rows[r:16:4]
                 )
 
-        def load_words(w, g):
+        def load_words(w, g, count=2):
             nc.sync.dma_start(
-                out=w_words[:, w, g : g + 2, :].bitcast(I32),
-                in_=all_words[w].bitcast(I32)[g : g + 2].rearrange("g p n -> p g n"),
+                out=w_words[:, w, g : g + count, :].bitcast(I32),
+                in_=all_words[w].bitcast(I32)[g : g + count].rearrange("g p n -> p g n"),
             )
 
         nc.sync.dma_start(out=volt_sb[:, 0, 0 : K // 2], in_=volt_rows[:, 0, 0 : K // 2])
         nc.sync.dma_start(out=volt_sb[:, 0, K // 2 : K], in_=volt_rows[:, 0, K // 2 : K])
         nc.sync.dma_start(out=volt_sb[:, 1, :], in_=volt_rows[:, 1, :])
         load_scales(0)
-        load_words(0, 0)
+        load_words(0, 0, 1)
+        load_words(0, 1, 1)
         load_words(0, 2)
         nc.sync.dma_start(out=loads_sb[:, 0, :], in_=loads_rows[:, 0, :])
         load_scales(1)

@@ -25,6 +25,7 @@ SAMPLE_TILES = B // P
 K_GROUPS = K // K_PASS
 COLUMN_HALVES = N // N_PASS
 WEIGHTS = 2
+BLOCK = 32
 PAIRS = PACK // 2
 
 PQ_VECTOR_COLS = (1280, 576)
@@ -62,8 +63,8 @@ def tile_kktloss_pc_kernel(
         v_planes = keep.tile([P, SAMPLE_TILES, K_GROUPS, P], U8, align_bytes=64)
         identity = keep.tile([P, P], F32)
         parts = keep.tile([P, SAMPLE_TILES, 2 * PART_COLS], F32)
-        totals = keep.tile([P, P], F32)
-        total_rows = keep.tile([P, P], F32)
+        totals = keep.tile([P, P], F32, align_bytes=64)
+        total_rows = keep.tile([P, P], F32, align_bytes=64)
         products = keep.tile([P, SAMPLE_TILES, COLUMN_HALVES, N_PASS], F32)
         differences = keep.tile([P, SAMPLE_TILES, K], F32)
         copies = keep.tile([P, SAMPLE_TILES, 2, K], BF16)
@@ -205,11 +206,13 @@ def tile_kktloss_pc_kernel(
                     pq_vector(1, 0, cv1, 2)
 
         nc.vector.tensor_reduce(
-            out=totals[:, 0:SAMPLE_TILES], in_=parts[:], axis=mybir.AxisListType.X, op=ALU.add
+            out=totals[:, 0 : BLOCK * SAMPLE_TILES : BLOCK],
+            in_=parts[:],
+            axis=mybir.AxisListType.X,
+            op=ALU.add,
         )
-        totals_flipped = psum_flip.tile([P, P], F32, tag="flip")
-        nc.tensor.transpose(totals_flipped[:], totals[:], identity[:])
-        nc.vector.tensor_copy(out=total_rows[:], in_=totals_flipped[:])
+        nc.vector.transpose(total_rows[:], totals[:])
         nc.sync.dma_start(
-            out=out.rearrange("(i p) -> i p", p=P), in_=total_rows[0:SAMPLE_TILES, :]
+            out=out.rearrange("(i q s) -> q i s", q=P // BLOCK, s=BLOCK),
+            in_=total_rows[0:P:BLOCK, 0 : BLOCK * SAMPLE_TILES].rearrange("q (i s) -> q i s", s=BLOCK),
         )

@@ -70,10 +70,17 @@ def tile_kktloss_pc_kernel(
         copies = keep.tile([P, SAMPLE_TILES, 2, K], BF16)
 
         nc.vector.memset(totals[:], 0.0)
-        for w in range(WEIGHTS):
-            nc.vector.memset(w_planes[w][:].bitcast(I32), 0)
+        nc.vector.memset(w_planes[0][:].bitcast(I32), 0)
         nc.vector.memset(parts[:], 0.0)
         masks.make_identity(nc, identity[:])
+        nc.gpsimd.memset(w_planes[1][:].bitcast(I32), 0)
+
+        def warm_up(count):
+            zeros = psum_flip.tile([P, P], F32, tag="flip")
+            for m in range(count):
+                nc.tensor.matmul(zeros[:], lhsT=totals[:], rhs=totals[:], start=(m == 0), stop=(m == count - 1))
+
+        warm_up(4)
 
 
         volt_rows = volt.rearrange("(i p) k -> p i k", p=P)
@@ -97,11 +104,12 @@ def tile_kktloss_pc_kernel(
 
         nc.sync.dma_start(out=volt_sb[:, 0, 0 : K // 2], in_=volt_rows[:, 0, 0 : K // 2])
         nc.sync.dma_start(out=volt_sb[:, 0, K // 2 : K], in_=volt_rows[:, 0, K // 2 : K])
-        nc.sync.dma_start(out=volt_sb[:, 1, :], in_=volt_rows[:, 1, :])
-        load_scales(0)
         load_words(0, 0, 1)
+        load_scales(0)
+        nc.sync.dma_start(out=volt_sb[:, 1, :], in_=volt_rows[:, 1, :])
         load_words(0, 1, 1)
-        load_words(0, 2)
+        load_words(0, 2, 1)
+        load_words(0, 3, 1)
         nc.sync.dma_start(out=loads_sb[:, 0, :], in_=loads_rows[:, 0, :])
         load_scales(1)
         load_words(1, 0)
@@ -111,8 +119,7 @@ def tile_kktloss_pc_kernel(
             nc.sync.dma_start(out=loads_sb[:, 1, cols], in_=loads_rows[:, 1, cols])
             nc.sync.dma_start(out=gens_sb[:, 1, cols], in_=gens_rows[:, 1, cols])
 
-        for n in range(SAMPLE_TILES * 2):
-            i, g0 = n // 2, 2 * (n % 2)
+        def quantise_half(i, g0):
             flipped = psum_flip.tile([P, 2, PAIRS, P], F32, tag="flip")
             for gg in range(2):
                 g = g0 + gg
@@ -124,7 +131,7 @@ def tile_kktloss_pc_kernel(
             side_by_side = (
                 volt_t[:, i, g0 : g0 + 2, :].bitcast(F32).rearrange("p g (b u) -> p g b u", u=PAIRS)
             )
-            if n % 2 == 0:
+            if g0 == 0:
                 nc.vector.tensor_copy(
                     out=side_by_side, in_=flipped[:].rearrange("p g u b -> p g b u")
                 )
@@ -176,10 +183,22 @@ def tile_kktloss_pc_kernel(
 
         landed = [(w, g) for w in range(WEIGHTS) for g in range(K_GROUPS)]
 
-        for w, g in landed[:-BANKWISE_LOADS]:
+        def load_passes(w, g, i):
+            for h in range(COLUMN_HALVES):
+                mx_pass(i, h, w, g)
+
+        quantise_half(0, 0)
+        quantise_half(0, 2)
+        load_passes(0, 0, 0)
+        quantise_half(1, 0)
+        quantise_half(1, 2)
+        for g in range(1, 3):
+            load_passes(0, g, 0)
+        for g in range(3):
+            load_passes(0, g, 1)
+        for w, g in landed[3:-BANKWISE_LOADS]:
             for i in range(SAMPLE_TILES):
-                for h in range(COLUMN_HALVES):
-                    mx_pass(i, h, w, g)
+                load_passes(w, g, i)
         cv0, cv1 = PQ_VECTOR_COLS
         pq_vector(0, 0, cv0, 2)
         pq_scalar(0, 0, cv0, K, 0)

@@ -28,10 +28,12 @@ WEIGHTS = 2
 BLOCK = 32
 PAIRS = PACK // 2
 
-PQ_VECTOR_COLS = (1280, 576)
 PQ_CUT = 1024
+PQ_PIECES = K // PQ_CUT
+assert PQ_PIECES == COLUMN_HALVES
+PQ_VECTOR_COLS = 448
 
-BANKWISE_LOADS = 3
+BANKWISE_LOADS = 4
 
 PART_COLS = 8
 VECTOR_PARTS = 0
@@ -80,8 +82,6 @@ def tile_kktloss_pc_kernel(
             for m in range(count):
                 nc.tensor.matmul(zeros[:], lhsT=totals[:], rhs=totals[:], start=(m == 0), stop=(m == count - 1))
 
-        warm_up(4)
-
 
         volt_rows = volt.rearrange("(i p) k -> p i k", p=P)
         loads_rows = pq_loads.rearrange("(i p) j -> p i j", p=P)
@@ -104,20 +104,20 @@ def tile_kktloss_pc_kernel(
 
         nc.sync.dma_start(out=volt_sb[:, 0, 0 : K // 2], in_=volt_rows[:, 0, 0 : K // 2])
         nc.sync.dma_start(out=volt_sb[:, 0, K // 2 : K], in_=volt_rows[:, 0, K // 2 : K])
+        nc.sync.dma_start(out=volt_sb[:, 1, 0 : K // 2], in_=volt_rows[:, 1, 0 : K // 2])
+        nc.sync.dma_start(out=volt_sb[:, 1, K // 2 : K], in_=volt_rows[:, 1, K // 2 : K])
         load_words(0, 0, 1)
         load_scales(0)
-        nc.sync.dma_start(out=volt_sb[:, 1, :], in_=volt_rows[:, 1, :])
         load_words(0, 1, 1)
         load_words(0, 2, 1)
         load_words(0, 3, 1)
-        nc.sync.dma_start(out=loads_sb[:, 0, :], in_=loads_rows[:, 0, :])
         load_scales(1)
         load_words(1, 0)
-        nc.sync.dma_start(out=gens_sb[:, 0, :], in_=gens_rows[:, 0, :])
         load_words(1, 2)
-        for cols in (slice(0, PQ_CUT), slice(PQ_CUT, K)):
-            nc.sync.dma_start(out=loads_sb[:, 1, cols], in_=loads_rows[:, 1, cols])
-            nc.sync.dma_start(out=gens_sb[:, 1, cols], in_=gens_rows[:, 1, cols])
+        for i in range(SAMPLE_TILES):
+            for cols in (slice(0, PQ_CUT), slice(PQ_CUT, K)):
+                nc.sync.dma_start(out=loads_sb[:, i, cols], in_=loads_rows[:, i, cols])
+                nc.sync.dma_start(out=gens_sb[:, i, cols], in_=gens_rows[:, i, cols])
 
         def quantise_half(i, g0):
             flipped = psum_flip.tile([P, 2, PAIRS, P], F32, tag="flip")
@@ -187,31 +187,31 @@ def tile_kktloss_pc_kernel(
             for h in range(COLUMN_HALVES):
                 mx_pass(i, h, w, g)
 
+        warm_up(3)
         quantise_half(0, 0)
         quantise_half(0, 2)
-        load_passes(0, 0, 0)
+        warm_up(1)
         quantise_half(1, 0)
         quantise_half(1, 2)
-        for g in range(1, 3):
-            load_passes(0, g, 0)
-        for g in range(3):
-            load_passes(0, g, 1)
-        for w, g in landed[3:-BANKWISE_LOADS]:
+        warm_up(2)
+        for i in range(SAMPLE_TILES):
+            for g in range(2):
+                load_passes(0, g, i)
+        for w, g in landed[2:-BANKWISE_LOADS]:
             for i in range(SAMPLE_TILES):
                 load_passes(w, g, i)
-        cv0, cv1 = PQ_VECTOR_COLS
-        pq_vector(0, 0, cv0, 2)
-        pq_scalar(0, 0, cv0, K, 0)
-        pq_scalar(1, 0, cv0, K, 1)
-        pq_scalar(0, 1, cv1, PQ_CUT, 2)
-        pq_scalar(1, 1, cv1, PQ_CUT, 3)
-        pq_scalar(0, 1, PQ_CUT, K, 4)
-        pq_scalar(1, 1, PQ_CUT, K, 5)
+        for i in range(SAMPLE_TILES):
+            for m in range(PQ_PIECES):
+                for which in range(2):
+                    pq_scalar(
+                        which, i, PQ_CUT * m + PQ_VECTOR_COLS, PQ_CUT * (m + 1), 2 * m + which
+                    )
 
         for i in range(SAMPLE_TILES):
             for h in range(COLUMN_HALVES):
                 for w, g in landed[-BANKWISE_LOADS:]:
                     mx_pass(i, h, w, g)
+                pq_vector(i, PQ_CUT * h, PQ_CUT * h + PQ_VECTOR_COLS, 2 + h)
                 nc.vector.scalar_tensor_tensor(
                     out=products[:, i, h, :],
                     in0=acc[(i, h)][:],
@@ -221,8 +221,6 @@ def tile_kktloss_pc_kernel(
                     op1=ALU.mult,
                     accum_out=parts[:, i, VECTOR_PARTS + h : VECTOR_PARTS + h + 1],
                 )
-                if (i, h) == (0, 0):
-                    pq_vector(1, 0, cv1, 2)
 
         nc.vector.tensor_reduce(
             out=totals[:, 0 : BLOCK * SAMPLE_TILES : BLOCK],

@@ -29,8 +29,6 @@ BLOCK = 32
 PAIRS = PACK // 2
 
 PQ_CUT = 1024
-PQ_PIECES = K // PQ_CUT
-assert PQ_PIECES == COLUMN_HALVES
 PQ_VECTOR_COLS = 448
 
 BANKWISE_LOADS = 4
@@ -104,20 +102,21 @@ def tile_kktloss_pc_kernel(
 
         nc.sync.dma_start(out=volt_sb[:, 0, 0 : K // 2], in_=volt_rows[:, 0, 0 : K // 2])
         nc.sync.dma_start(out=volt_sb[:, 0, K // 2 : K], in_=volt_rows[:, 0, K // 2 : K])
-        nc.sync.dma_start(out=volt_sb[:, 1, 0 : K // 2], in_=volt_rows[:, 1, 0 : K // 2])
-        nc.sync.dma_start(out=volt_sb[:, 1, K // 2 : K], in_=volt_rows[:, 1, K // 2 : K])
+        nc.sync.dma_start(out=volt_sb[:, 1, :], in_=volt_rows[:, 1, :])
         load_words(0, 0, 1)
         load_scales(0)
         load_words(0, 1, 1)
-        load_words(0, 2, 1)
-        load_words(0, 3, 1)
+        load_words(0, 2)
         load_scales(1)
         load_words(1, 0)
         load_words(1, 2)
-        for i in range(SAMPLE_TILES):
-            for cols in (slice(0, PQ_CUT), slice(PQ_CUT, K)):
-                nc.sync.dma_start(out=loads_sb[:, i, cols], in_=loads_rows[:, i, cols])
-                nc.sync.dma_start(out=gens_sb[:, i, cols], in_=gens_rows[:, i, cols])
+        pieces = (slice(0, PQ_CUT), slice(PQ_CUT, K))
+        for cols in pieces:
+            nc.sync.dma_start(out=loads_sb[:, 0, cols], in_=loads_rows[:, 0, cols])
+            nc.sync.dma_start(out=gens_sb[:, 0, cols], in_=gens_rows[:, 0, cols])
+        nc.sync.dma_start(out=loads_sb[:, 1, :], in_=loads_rows[:, 1, :])
+        for cols in pieces:
+            nc.sync.dma_start(out=gens_sb[:, 1, cols], in_=gens_rows[:, 1, cols])
 
         def quantise_half(i, g0):
             flipped = psum_flip.tile([P, 2, PAIRS, P], F32, tag="flip")
@@ -187,31 +186,26 @@ def tile_kktloss_pc_kernel(
             for h in range(COLUMN_HALVES):
                 mx_pass(i, h, w, g)
 
-        warm_up(3)
-        quantise_half(0, 0)
-        quantise_half(0, 2)
-        warm_up(1)
-        quantise_half(1, 0)
-        quantise_half(1, 2)
-        warm_up(2)
+        warm_up(4)
+        for i in range(SAMPLE_TILES):
+            for g in range(0, K_GROUPS, 2):
+                quantise_half(i, g)
         for i in range(SAMPLE_TILES):
             for g in range(2):
                 load_passes(0, g, i)
         for w, g in landed[2:-BANKWISE_LOADS]:
             for i in range(SAMPLE_TILES):
                 load_passes(w, g, i)
-        for i in range(SAMPLE_TILES):
-            for m in range(PQ_PIECES):
-                for which in range(2):
-                    pq_scalar(
-                        which, i, PQ_CUT * m + PQ_VECTOR_COLS, PQ_CUT * (m + 1), 2 * m + which
-                    )
+        for which in range(4):
+            m = which // 2
+            pq_scalar(which % 2, 0, PQ_CUT * m + PQ_VECTOR_COLS, PQ_CUT * (m + 1), which)
+        pq_scalar(0, 1, PQ_CUT, K, 0)
+        pq_scalar(1, 1, PQ_CUT, K, 1)
 
         for i in range(SAMPLE_TILES):
             for h in range(COLUMN_HALVES):
                 for w, g in landed[-BANKWISE_LOADS:]:
                     mx_pass(i, h, w, g)
-                pq_vector(i, PQ_CUT * h, PQ_CUT * h + PQ_VECTOR_COLS, 2 + h)
                 nc.vector.scalar_tensor_tensor(
                     out=products[:, i, h, :],
                     in0=acc[(i, h)][:],
@@ -221,6 +215,10 @@ def tile_kktloss_pc_kernel(
                     op1=ALU.mult,
                     accum_out=parts[:, i, VECTOR_PARTS + h : VECTOR_PARTS + h + 1],
                 )
+                if i == 0:
+                    pq_vector(0, PQ_CUT * h, PQ_CUT * h + PQ_VECTOR_COLS, 2 + h)
+                elif h == 0:
+                    pq_vector(1, 0, PQ_CUT, 2)
 
         nc.vector.tensor_reduce(
             out=totals[:, 0 : BLOCK * SAMPLE_TILES : BLOCK],

@@ -26,12 +26,13 @@ K_GROUPS = K // K_PASS
 COLUMN_HALVES = N // N_PASS
 WEIGHTS = 2
 BLOCK = 32
+HALF_K = K // 2
 PAIRS = PACK // 2
 
 PQ_CUT = 1024
 PQ_VECTOR_COLS = 448
 
-BANKWISE_LOADS = 4
+BANKWISE_LOADS = 5
 
 PART_COLS = 8
 VECTOR_PARTS = 0
@@ -50,7 +51,7 @@ def tile_kktloss_pc_kernel(
         psum_acc = ctx.enter_context(tc.psum_pool(name="psum_acc", bufs=1))
         ctx.enter_context(tc.manual_schedule())
 
-        volt_sb = keep.tile([P, SAMPLE_TILES, K], BF16)
+        volt_sb = keep.tile([P, 2, SAMPLE_TILES, HALF_K], BF16)
         loads_sb = keep.tile([P, SAMPLE_TILES, K], BF16)
         gens_sb = keep.tile([P, SAMPLE_TILES, K], BF16)
         w_words = keep.tile([P, WEIGHTS, K_GROUPS, 2 * N], U8, align_bytes=64)
@@ -100,16 +101,18 @@ def tile_kktloss_pc_kernel(
                 in_=all_words[w].bitcast(I32)[g : g + count].rearrange("g p n -> p g n"),
             )
 
-        nc.sync.dma_start(out=volt_sb[:, 0, 0 : K // 2], in_=volt_rows[:, 0, 0 : K // 2])
-        nc.sync.dma_start(out=volt_sb[:, 0, K // 2 : K], in_=volt_rows[:, 0, K // 2 : K])
-        nc.sync.dma_start(out=volt_sb[:, 1, :], in_=volt_rows[:, 1, :])
+        for half in range(2):
+            nc.sync.dma_start(
+                out=volt_sb[:, half], in_=volt_rows[:, :, HALF_K * half : HALF_K * (half + 1)]
+            )
         load_words(0, 0, 1)
         load_scales(0)
         load_words(0, 1, 1)
         load_words(0, 2)
         load_scales(1)
         load_words(1, 0)
-        load_words(1, 2)
+        load_words(1, 2, 1)
+        load_words(1, 3, 1)
         pieces = (slice(0, PQ_CUT), slice(PQ_CUT, K))
         for cols in pieces:
             nc.sync.dma_start(out=loads_sb[:, 0, cols], in_=loads_rows[:, 0, cols])
@@ -122,7 +125,7 @@ def tile_kktloss_pc_kernel(
             flipped = psum_flip.tile([P, 2, PAIRS, P], F32, tag="flip")
             for gg in range(2):
                 g = g0 + gg
-                volt_pairs = volt_sb[:, i, K_PASS * g : K_PASS * (g + 1)].bitcast(F32)
+                volt_pairs = volt_sb[:, g0 // 2, i, K_PASS * gg : K_PASS * (gg + 1)].bitcast(F32)
                 for u in range(PAIRS):
                     nc.tensor.transpose(
                         flipped[:, gg, u, :], volt_pairs[:, u : K_PASS // 2 : PAIRS], identity[:]
@@ -130,7 +133,7 @@ def tile_kktloss_pc_kernel(
             side_by_side = (
                 volt_t[:, i, g0 : g0 + 2, :].bitcast(F32).rearrange("p g (b u) -> p g b u", u=PAIRS)
             )
-            if g0 == 0:
+            if i == 0:
                 nc.vector.tensor_copy(
                     out=side_by_side, in_=flipped[:].rearrange("p g u b -> p g b u")
                 )
@@ -187,8 +190,8 @@ def tile_kktloss_pc_kernel(
                 mx_pass(i, h, w, g)
 
         warm_up(4)
-        for i in range(SAMPLE_TILES):
-            for g in range(0, K_GROUPS, 2):
+        for g in range(0, K_GROUPS, 2):
+            for i in range(SAMPLE_TILES):
                 quantise_half(i, g)
         for i in range(SAMPLE_TILES):
             for g in range(2):
@@ -210,7 +213,7 @@ def tile_kktloss_pc_kernel(
                     out=products[:, i, h, :],
                     in0=acc[(i, h)][:],
                     scalar=1.0,
-                    in1=volt_sb[:, i, N_PASS * h : N_PASS * (h + 1)],
+                    in1=volt_sb[:, 0, i, N_PASS * h : N_PASS * (h + 1)],
                     op0=ALU.mult,
                     op1=ALU.mult,
                     accum_out=parts[:, i, VECTOR_PARTS + h : VECTOR_PARTS + h + 1],

from contextlib import ExitStack

import concourse.masks as masks
import concourse.mybir as mybir

BF16 = mybir.dt.bfloat16
F32 = mybir.dt.float32
I32 = mybir.dt.int32
U8 = mybir.dt.uint8
U32 = mybir.dt.uint32
FP8X4 = mybir.dt.float8_e4m3fn_x4
FP4X4 = mybir.dt.float4_e2m1fn_x4
ALU = mybir.AluOpType
COPY = mybir.ActivationFunctionType.Copy

P = 128
PACK = 4
K_PASS = P * PACK
B = 256
K = 2048
N = 1024
N_PASS = 512
assert N_PASS == K_PASS
SAMPLE_TILES = B // P
K_GROUPS = K // K_PASS
COLUMN_HALVES = N // N_PASS
WEIGHTS = 2
BLOCK = 32
HALF_K = K // 2
PAIRS = PACK // 2

PQ_CUT = 1024
PQ_VECTOR_COLS = 448

BANKWISE_LOADS = 5

PART_COLS = 8
VECTOR_PARTS = 0
SCALAR_PARTS = PART_COLS

FLOPS = 2 * B * K * N * WEIGHTS


def tile_kktloss_pc_kernel(
    tc, volt, y_words, y_scales, yc_words, yc_scales, pq_loads, pq_gens, out
):
    nc = tc.nc
    with ExitStack() as ctx:
        keep = ctx.enter_context(tc.tile_pool(name="keep", bufs=1))
        psum_flip = ctx.enter_context(tc.psum_pool(name="psum_flip", bufs=K_GROUPS))
        psum_acc = ctx.enter_context(tc.psum_pool(name="psum_acc", bufs=1))
        ctx.enter_context(tc.manual_schedule())

        volt_sb = keep.tile([P, 2, SAMPLE_TILES, HALF_K], BF16)
        loads_sb = keep.tile([P, SAMPLE_TILES, K], BF16)
        gens_sb = keep.tile([P, SAMPLE_TILES, K], BF16)
        w_words = keep.tile([P, WEIGHTS, K_GROUPS, 2 * N], U8, align_bytes=64)
        w_planes = [
            keep.tile([P, K_GROUPS, N], U8, align_bytes=64, name="w_planes_%d" % w)
            for w in range(WEIGHTS)
        ]
        volt_t = keep.tile([P, SAMPLE_TILES, K_GROUPS, P * PACK], BF16, align_bytes=64)
        v_words = keep.tile([P, SAMPLE_TILES, K_GROUPS, P], U32, align_bytes=64)
        v_planes = keep.tile([P, SAMPLE_TILES, K_GROUPS, P], U8, align_bytes=64)
        identity = keep.tile([P, P], F32)
        parts = keep.tile([P, SAMPLE_TILES, 2 * PART_COLS], F32)
        totals = keep.tile([P, P], F32, align_bytes=64)
        total_rows = keep.tile([P, P], F32, align_bytes=64)
        products = keep.tile([P, SAMPLE_TILES, COLUMN_HALVES, N_PASS], F32)
        differences = keep.tile([P, SAMPLE_TILES, K], F32)
        copies = keep.tile([P, SAMPLE_TILES, 2, K], BF16)

        nc.vector.memset(totals[:], 0.0)
        nc.vector.memset(w_planes[0][:].bitcast(I32), 0)
        nc.vector.memset(parts[:], 0.0)
        masks.make_identity(nc, identity[:])
        nc.gpsimd.memset(w_planes[1][:].bitcast(I32), 0)

        def warm_up(count):
            zeros = psum_flip.tile([P, P], F32, tag="flip")
            for m in range(count):
                nc.tensor.matmul(zeros[:], lhsT=totals[:], rhs=totals[:], start=(m == 0), stop=(m == count - 1))


        volt_rows = volt.rearrange("(i p) k -> p i k", p=P)
        loads_rows = pq_loads.rearrange("(i p) j -> p i j", p=P)
        gens_rows = pq_gens.rearrange("(i p) j -> p i j", p=P)
        all_words = (y_words, yc_words)
        all_scales = (y_scales, yc_scales)

        def load_scales(w):
            scale_rows = all_scales[w].bitcast(I32).rearrange("g q n -> q g n")
            for r in range(4):
                nc.sync.dma_start(
                    out=w_planes[w][r:P:32].bitcast(I32), in_=scale_rows[r:16:4]
                )

        def load_words(w, g, count=2):
            nc.sync.dma_start(
                out=w_words[:, w, g : g + count, :].bitcast(I32),
                in_=all_words[w].bitcast(I32)[g : g + count].rearrange("g p n -> p g n"),
            )

        for half in range(2):
            nc.sync.dma_start(
                out=volt_sb[:, half], in_=volt_rows[:, :, HALF_K * half : HALF_K * (half + 1)]
            )
        load_words(0, 0, 1)
        load_scales(0)
        load_words(0, 1, 1)
        load_words(0, 2)
        load_scales(1)
        load_words(1, 0)
        load_words(1, 2, 1)
        load_words(1, 3, 1)
        pieces = (slice(0, PQ_CUT), slice(PQ_CUT, K))
        for cols in pieces:
            nc.sync.dma_start(out=loads_sb[:, 0, cols], in_=loads_rows[:, 0, cols])
            nc.sync.dma_start(out=gens_sb[:, 0, cols], in_=gens_rows[:, 0, cols])
        nc.sync.dma_start(out=loads_sb[:, 1, :], in_=loads_rows[:, 1, :])
        for cols in pieces:
            nc.sync.dma_start(out=gens_sb[:, 1, cols], in_=gens_rows[:, 1, cols])

        def quantise_half(i, g0):
            flipped = psum_flip.tile([P, 2, PAIRS, P], F32, tag="flip")
            for gg in range(2):
                g = g0 + gg
                volt_pairs = volt_sb[:, g0 // 2, i, K_PASS * gg : K_PASS * (gg + 1)].bitcast(F32)
                for u in range(PAIRS):
                    nc.tensor.transpose(
                        flipped[:, gg, u, :], volt_pairs[:, u : K_PASS // 2 : PAIRS], identity[:]
                    )
            side_by_side = (
                volt_t[:, i, g0 : g0 + 2, :].bitcast(F32).rearrange("p g (b u) -> p g b u", u=PAIRS)
            )
            if i == 0:
                nc.vector.tensor_copy(
                    out=side_by_side, in_=flipped[:].rearrange("p g u b -> p g b u")
                )
            else:
                nc.scalar.copy(
                    out=side_by_side, in_=flipped[:].rearrange("p g u b -> p g b u")
                )
            nc.vector.quantize_mx(
                out=v_words[:, i, g0 : g0 + 2, :].rearrange("p g b -> p (g b)").bitcast(FP8X4),
                scales=v_planes[:, i, g0 : g0 + 2, :].rearrange("p g b -> p (g b)"),
                in_=volt_t[:, i, g0 : g0 + 2, :].rearrange("p g c -> p (g c)"),
            )

        acc = {}
        for i in range(SAMPLE_TILES):
            for h in range(COLUMN_HALVES):
                acc[(i, h)] = psum_acc.tile([P, N_PASS], F32, name="acc_%d_%d" % (i, h))

        def mx_pass(i, h, w, g):
            nc.tensor.matmul_mx(
                out=acc[(i, h)][:],
                lhsT=v_words[:, i, g, :].bitcast(FP8X4),
                lhsT_scale=v_planes[:, i, g, :],
                rhs=w_words[:, w, g, 2 * N_PASS * h : 2 * N_PASS * (h + 1)].bitcast(FP4X4),
                rhs_scale=w_planes[w][:, g, N_PASS * h : N_PASS * (h + 1)],
                start=(w == 0 and g == 0),
                stop=(w == WEIGHTS - 1 and g == K_GROUPS - 1),
            )

        def pq_vector(i, c0, c1, slot):
            nc.vector.scalar_tensor_tensor(
                out=differences[:, i, c0:c1],
                in0=loads_sb[:, i, c0:c1],
                scalar=1.0,
                in1=gens_sb[:, i, c0:c1],
                op0=ALU.mult,
                op1=ALU.subtract,
                accum_out=parts[:, i, VECTOR_PARTS + slot : VECTOR_PARTS + slot + 1],
            )

        def pq_scalar(which, i, c0, c1, slot):
            nc.scalar.activation(
                out=copies[:, i, which, c0:c1],
                in_=(loads_sb, gens_sb)[which][:, i, c0:c1],
                func=COPY,
                scale=(1.0, -1.0)[which],
                accum_out=parts[:, i, SCALAR_PARTS + slot : SCALAR_PARTS + slot + 1],
            )

        landed = [(w, g) for w in range(WEIGHTS) for g in range(K_GROUPS)]

        def load_passes(w, g, i):
            for h in range(COLUMN_HALVES):
                mx_pass(i, h, w, g)

        warm_up(4)
        for g in range(0, K_GROUPS, 2):
            for i in range(SAMPLE_TILES):
                quantise_half(i, g)
        for i in range(SAMPLE_TILES):
            for g in range(2):
                load_passes(0, g, i)
        for w, g in landed[2:-BANKWISE_LOADS]:
            for i in range(SAMPLE_TILES):
                load_passes(w, g, i)
        for which in range(4):
            m = which // 2
            pq_scalar(which % 2, 0, PQ_CUT * m + PQ_VECTOR_COLS, PQ_CUT * (m + 1), which)
        pq_scalar(0, 1, PQ_CUT, K, 0)
        pq_scalar(1, 1, PQ_CUT, K, 1)

        for i in range(SAMPLE_TILES):
            for h in range(COLUMN_HALVES):
                for w, g in landed[-BANKWISE_LOADS:]:
                    mx_pass(i, h, w, g)
                nc.vector.scalar_tensor_tensor(
                    out=products[:, i, h, :],
                    in0=acc[(i, h)][:],
                    scalar=1.0,
                    in1=volt_sb[:, 0, i, N_PASS * h : N_PASS * (h + 1)],
                    op0=ALU.mult,
                    op1=ALU.mult,
                    accum_out=parts[:, i, VECTOR_PARTS + h : VECTOR_PARTS + h + 1],
                )
                if i == 0:
                    pq_vector(0, PQ_CUT * h, PQ_CUT * h + PQ_VECTOR_COLS, 2 + h)
                elif h == 0:
                    pq_vector(1, 0, PQ_CUT, 2)

        nc.vector.tensor_reduce(
            out=totals[:, 0 : BLOCK * SAMPLE_TILES : BLOCK],
            in_=parts[:],
            axis=mybir.AxisListType.X,
            op=ALU.add,
        )
        nc.vector.transpose(total_rows[:], totals[:])
        nc.sync.dma_start(
            out=out.rearrange("(i q s) -> q i s", q=P // BLOCK, s=BLOCK),
            in_=total_rows[0:P:BLOCK, 0 : BLOCK * SAMPLE_TILES].rearrange("q (i s) -> q i s", s=BLOCK),
        )
